import numpy as np
import ml_dtypes


def mxq(x, axis, fmt="e4m3"):
    dtype, down = {"e4m3": (ml_dtypes.float8_e4m3fn, 7), "e5m2": (ml_dtypes.float8_e5m2, 14)}[fmt]
    v = np.moveaxis(np.asarray(x, np.float32).astype(ml_dtypes.bfloat16).astype(np.float64), axis, -1)
    blocks = v.reshape(v.shape[:-1] + (-1, 32))
    amax = np.abs(blocks).max(-1, keepdims=True)
    byte = np.maximum(np.where(amax > 0, np.frexp(amax)[1] - 1 + 127, 0) - down, 1)
    scale = np.exp2(byte - 127.0)
    codes = (blocks / scale).astype(np.float32).astype(dtype).astype(np.float64)
    return np.moveaxis((codes * scale).reshape(v.shape), -1, axis)


WIDE = False


def mx_kscale(k):
    if not WIDE:
        return np.ones(k)
    levels = np.array([10, -10, 5, -5, 0])
    a = np.random.permutation(np.resize(levels, k // 512 * 4)).reshape(k // 512, 4)
    idx = np.arange(k)
    return np.exp2(a[idx // 512, idx % 128 // 32])


BF16 = ml_dtypes.bfloat16


def bf(x):
    return np.asarray(x, np.float32).astype(BF16)


def f64(x):
    return np.asarray(x).astype(np.float64)


E2M1 = np.array([0.0, 0.5, 1.0, 1.5, 2.0, 3.0, 4.0, 6.0, -0.0, -0.5, -1.0, -1.5, -2.0, -3.0, -4.0, -6.0])


def pack_weight(w, fmt):
    k, n = w.shape
    w = f64(bf(w)).reshape(k // 32, 32, n)
    amax = np.abs(w).max(1)
    if fmt == "e4m3":
        byte = np.frexp(amax)[1] - 1 + 127 - 7
    else:
        mant, ex = np.frexp(amax / 6.0)
        byte = np.where(mant > 0.5, ex, ex - 1) + 127
    byte = np.clip(np.where(amax > 0, byte, 1), 1, 254)
    scaled = (w * np.exp2(127.0 - byte)[:, None, :]).reshape(k, n).astype(np.float32)
    by_word = np.ascontiguousarray(scaled.reshape(k // 512, 128, 4, n).transpose(0, 1, 3, 2))
    if fmt == "e4m3":
        words = by_word.astype(ml_dtypes.float8_e4m3fn).view(np.uint8)
    else:
        c = by_word.astype(ml_dtypes.float4_e2m1fn).view(np.uint8) & 0xF
        words = c[..., 0::2] | (c[..., 1::2] << 4)
    return np.ascontiguousarray(words), np.ascontiguousarray(byte.astype(np.uint8).reshape(k // 512, 16, n))


def unpack_weight(words, scales, fmt):
    g, p, n, _ = words.shape
    if fmt == "e4m3":
        vals = np.ascontiguousarray(words).view(ml_dtypes.float8_e4m3fn).astype(np.float64)
    else:
        nib = np.empty((g, p, n, 4), np.uint8)
        nib[..., 0::2] = words & 0xF
        nib[..., 1::2] = words >> 4
        vals = E2M1[nib]
    vals = vals * np.repeat(np.exp2(scales.astype(np.float64) - 127.0), 8, axis=1)[..., None]
    return vals.transpose(0, 1, 3, 2).reshape(g * 512, n)

def pack4(w):
    words, scales = pack_weight(w, "e2m1")
    return words.reshape(words.shape[0], 128, -1), scales


def unpack4(words, scales):
    return unpack_weight(words.reshape(words.shape[0], 128, -1, 2), scales, "e2m1")


B, S, DIM, H, NOPE, ROPE, VHD, KV_RANK = 2, 64, 512, 16, 128, 64, 128, 512
QKHD = NOPE + ROPE
HALF = ROPE // 2


def rope(u, cos, sin):
    ur = u.reshape(u.shape[:-1] + (HALF, 2))
    a, b = ur[..., 0], ur[..., 1]
    c = cos[None, :, None, :]
    s = sin[None, :, None, :]
    return np.stack([a * c - b * s, a * s + b * c], axis=-1).reshape(u.shape)


def setup_inputs():
    s = mx_kscale(DIM)
    inv_freq = 1.0 / 10000.0 ** (np.arange(0, ROPE, 2) / ROPE)
    ang = np.arange(S)[:, None] * inv_freq[None, :]
    x = bf(np.random.standard_normal((B, S, DIM)) * s)
    wq_w_words, wq_w_scales = pack4(np.random.standard_normal((DIM, H * QKHD)) / np.sqrt(DIM) / s[:, None])
    return {"x": x,
            "wq_w_words": wq_w_words, "wq_w_scales": wq_w_scales,
            "wq_b": bf(np.random.standard_normal(H * QKHD) * 0.2),
            "cos": bf(np.cos(ang)), "sin": bf(np.sin(ang))}


def reference(x, wq_w_words, wq_w_scales, wq_b, cos, sin):
    q = (mxq(f64(x), 2, "e4m3") @ unpack4(wq_w_words, wq_w_scales)) + f64(wq_b)
    q = q.reshape(B, S, H, QKHD)
    return np.concatenate([q[..., :NOPE], rope(q[..., NOPE:], f64(cos), f64(sin))], axis=-1)

@@ -1,0 +1,206 @@
+from contextlib import ExitStack
+
+import concourse.mybir as mybir
+from concourse.masks import make_identity
+
+F32 = mybir.dt.float32
+BF16 = mybir.dt.bfloat16
+I32 = mybir.dt.int32
+U32 = mybir.dt.uint32
+U8 = mybir.dt.uint8
+FP8X4 = mybir.dt.float8_e4m3fn_x4
+FP4X4 = mybir.dt.float4_e2m1fn_x4
+ADD = mybir.AluOpType.add
+MULT = mybir.AluOpType.mult
+
+P = 128
+BATCH = 2
+SEQ = 64
+DIM = 512
+HEADS = 16
+NOPE = 128
+ROPE = 64
+HALF = ROPE // 2
+HEAD = NOPE + ROPE
+COLS = HEADS * HEAD
+
+GROUPS = 4
+GROUP_HEADS = HEADS // GROUPS
+GROUP_COLS = GROUP_HEADS * HEAD
+BANK_HEADS = 2
+BANK_COLS = BANK_HEADS * HEAD
+BANKS = GROUP_HEADS // BANK_HEADS
+PASSES = ((0, 256), (256, 128))
+GROUP_WORDS = GROUP_COLS // 2
+WORD_PLANES = GROUP_WORDS // P
+
+BIAS_AHEAD = 2
+
+FLOPS = 2 * P * DIM * COLS
+
+
+def tile_mla_pb_s_kernel(tc, x, wq_w_words, wq_w_scales, wq_b, cos, sin, out):
+    nc = tc.nc
+    x_rows = x.rearrange("b s k -> (b s) k")
+    w_rows = wq_w_words.rearrange("g p c -> (g p) c")
+    scale_rows = wq_w_scales.rearrange("g q n -> (g q) n")
+    out_rows = out.rearrange("b s h d -> (b s) (h d)")
+
+    with ExitStack() as stack:
+        keep = stack.enter_context(tc.tile_pool(name="keep", bufs=1))
+        group = stack.enter_context(tc.tile_pool(name="group", bufs=GROUPS))
+        xt_bank = stack.enter_context(tc.psum_pool(name="xt_bank", bufs=1))
+        bias_banks = stack.enter_context(tc.psum_pool(name="bias_banks", bufs=BIAS_AHEAD))
+        acc_banks = stack.enter_context(tc.psum_pool(name="acc_banks", bufs=2 * BANKS))
+        stack.enter_context(tc.manual_schedule())
+
+        identity = keep.tile([P, P], F32)
+        nc.vector.memset(identity[:], 0.0)
+        make_identity(nc, identity[:], nomemset=True)
+
+        cos_sin_bf = keep.tile([P, 2, HALF], BF16)
+        for plane, table in enumerate((cos, sin)):
+            nc.gpsimd.dma_start(
+                out=cos_sin_bf[:, plane, :],
+                in_=table.unsqueeze(0).to_broadcast([BATCH, SEQ, HALF]),
+            )
+
+        x_sb = keep.tile([P, DIM], BF16)
+        nc.sync.dma_start(out=x_sb[:], in_=x_rows)
+
+        b_sb = keep.tile([P, GROUPS, 2 * WORD_PLANES], BF16)
+        nc.scalar.dma_start(
+            out=b_sb[:], in_=wq_b.rearrange("(g p e) -> p g e", g=GROUPS, p=P)
+        )
+
+        w_scales = keep.tile([P, COLS], U8, align_bytes=64)
+        nc.vector.memset(w_scales[:].bitcast(I32), 0)
+        for r in range(4):
+            nc.sync.dma_start(
+                out=w_scales[r:P:32, :].bitcast(I32),
+                in_=scale_rows[r:16:4, :].bitcast(I32),
+            )
+
+        w_words = keep.tile([P, 2 * COLS], U8, align_bytes=64)
+        for g in range(GROUPS):
+            group_bytes = slice(2 * GROUP_COLS * g, 2 * GROUP_COLS * (g + 1))
+            nc.sync.dma_start(
+                out=w_words[:, group_bytes].bitcast(I32),
+                in_=w_rows[:, group_bytes].bitcast(I32),
+            )
+
+        x_words = x_sb[:].bitcast(F32)
+        xt = xt_bank.tile([P, 2, P], F32)
+        for u in range(2):
+            nc.tensor.transpose(xt[:, u, :], x_words[:, u : DIM // 2 : 2], identity[:])
+        x_grouped = keep.tile([P, P, 4], BF16, align_bytes=64)
+        nc.scalar.copy(out=x_grouped[:].bitcast(F32), in_=xt[:].rearrange("p u r -> p r u"))
+        x_codes = keep.tile([P, P], U32, align_bytes=64)
+        x_scales = keep.tile([P, P], U8, align_bytes=64)
+        nc.vector.quantize_mx(
+            out=x_codes[:].bitcast(FP8X4),
+            scales=x_scales[:],
+            in_=x_grouped[:].rearrange("p r t -> p (r t)"),
+        )
+
+        b_words = b_sb[:].bitcast(F32)
+
+        def spread_bias(g):
+            spread = bias_banks.tile([P, WORD_PLANES, P], F32)
+            for w in range(WORD_PLANES):
+                nc.tensor.transpose(
+                    spread[:, w, :], b_words[:, g, w : w + 1].to_broadcast([P, P]), identity[:]
+                )
+            bias = group.tile([P, GROUP_HEADS, HEAD], BF16)
+            nc.scalar.copy(
+                out=bias[:]
+                .rearrange("p h d -> p (h d)")
+                .bitcast(F32)
+                .rearrange("p (n w) -> p n w", w=WORD_PLANES),
+                in_=spread[:].rearrange("p w n -> p n w"),
+            )
+            return bias
+
+        def multiply(g, bank):
+            first = GROUP_COLS * g + BANK_COLS * bank
+            acc = acc_banks.tile([P, BANK_HEADS, HEAD], F32)
+            acc_cols = acc[:].rearrange("p h d -> p (h d)")
+            for offset, width in PASSES:
+                col = first + offset
+                nc.tensor.matmul_mx(
+                    out=acc_cols[:, offset : offset + width],
+                    lhsT=x_codes[:].bitcast(FP8X4),
+                    lhsT_scale=x_scales[:],
+                    rhs=w_words[:, 2 * col : 2 * (col + width)].bitcast(FP4X4),
+                    rhs_scale=w_scales[:, col : col + width],
+                    start=True,
+                    stop=True,
+                )
+            return acc
+
+        biases = [spread_bias(g) for g in range(BIAS_AHEAD)]
+
+        cos_cos = keep.tile([P, 2, HALF], F32)
+        nc.scalar.copy(
+            out=cos_cos[:], in_=cos_sin_bf[:, 0:1, :].to_broadcast([P, 2, HALF])
+        )
+        sin_sin = keep.tile([P, 2, HALF], F32)
+        nc.scalar.mul(out=sin_sin[:, 0, :], in_=cos_sin_bf[:, 1, :], mul=-1.0)
+        nc.scalar.copy(out=sin_sin[:, 1, :], in_=cos_sin_bf[:, 1, :])
+        planes_shape = [P, GROUP_HEADS, 2, HALF]
+        plane_shape = [P, GROUP_HEADS, HALF]
+
+        for g in range(GROUPS):
+            accs = [multiply(g, bank) for bank in range(BANKS)]
+            bias = biases[g]
+            bank_heads = [slice(BANK_HEADS * bank, BANK_HEADS * (bank + 1)) for bank in range(BANKS)]
+
+            q = group.tile([P, GROUP_HEADS, HEAD], F32)
+            planes = group.tile([P, GROUP_HEADS, 2, HALF], F32)
+            for bank in range(BANKS):
+                nc.vector.tensor_tensor(
+                    out=planes[:, bank_heads[bank], :, :],
+                    in0=accs[bank][:, :, NOPE:HEAD].rearrange("p h (j t) -> p h t j", t=2),
+                    in1=bias[:, bank_heads[bank], NOPE:HEAD].rearrange("p h (j t) -> p h t j", t=2),
+                    op=ADD,
+                )
+            nc.scalar.copy(out=q[:, bank_heads[1], 0:NOPE], in_=accs[1][:, :, 0:NOPE])
+            if g + BIAS_AHEAD < GROUPS:
+                biases.append(spread_bias(g + BIAS_AHEAD))
+            nc.vector.tensor_tensor(
+                out=q[:, bank_heads[0], 0:NOPE],
+                in0=accs[0][:, :, 0:NOPE],
+                in1=bias[:, bank_heads[0], 0:NOPE],
+                op=ADD,
+            )
+            nc.gpsimd.tensor_tensor(
+                out=q[:, bank_heads[1], 0:NOPE],
+                in0=q[:, bank_heads[1], 0:NOPE],
+                in1=bias[:, bank_heads[1], 0:NOPE],
+                op=ADD,
+            )
+            crossed = group.tile(planes_shape, F32)
+            for t in range(2):
+                nc.vector.tensor_tensor(
+                    out=crossed[:, :, t, :],
+                    in0=planes[:, :, 1 - t, :],
+                    in1=sin_sin[:, t : t + 1, :].to_broadcast(plane_shape),
+                    op=MULT,
+                )
+            straight = group.tile(planes_shape, F32)
+            nc.vector.tensor_tensor(
+                out=straight[:],
+                in0=planes[:],
+                in1=cos_cos[:].unsqueeze(1).to_broadcast(planes_shape),
+                op=MULT,
+            )
+            nc.vector.tensor_tensor(
+                out=q[:, :, NOPE:HEAD].rearrange("p h (j t) -> p h j t", t=2),
+                in0=straight[:].rearrange("p h t j -> p h j t"),
+                in1=crossed[:].rearrange("p h t j -> p h j t"),
+                op=ADD,
+            )
+            nc.sync.dma_start(
+                out=out_rows[:, GROUP_COLS * g : GROUP_COLS * (g + 1)],
+                in_=q[:].rearrange("p h d -> p (h d)"),
+            )

@@ -59,11 +59,6 @@ def tile_mla_pb_s_kernel(tc, x, wq_w_words, wq_w_scales, wq_b, cos, sin, out):
         make_identity(nc, identity[:], nomemset=True)
 
         cos_sin_bf = keep.tile([P, 2, HALF], BF16)
-        for plane, table in enumerate((cos, sin)):
-            nc.gpsimd.dma_start(
-                out=cos_sin_bf[:, plane, :],
-                in_=table.unsqueeze(0).to_broadcast([BATCH, SEQ, HALF]),
-            )
 
         x_sb = keep.tile([P, DIM], BF16)
         nc.sync.dma_start(out=x_sb[:], in_=x_rows)
@@ -87,6 +82,12 @@ def tile_mla_pb_s_kernel(tc, x, wq_w_words, wq_w_scales, wq_b, cos, sin, out):
             nc.sync.dma_start(
                 out=w_words[:, group_bytes].bitcast(I32),
                 in_=w_rows[:, group_bytes].bitcast(I32),
+            )
+
+        for plane, table in enumerate((cos, sin)):
+            nc.sync.dma_start(
+                out=cos_sin_bf[:, plane, :],
+                in_=table.unsqueeze(0).to_broadcast([BATCH, SEQ, HALF]),
             )
 
         x_words = x_sb[:].bitcast(F32)

@@ -49,17 +49,25 @@ def tile_mla_pb_s_kernel(tc, x, wq_w_words, wq_w_scales, wq_b, cos, sin, out):
     with ExitStack() as stack:
         keep = stack.enter_context(tc.tile_pool(name="keep", bufs=1))
         group = stack.enter_context(tc.tile_pool(name="group", bufs=GROUPS))
-        xt_bank = stack.enter_context(tc.psum_pool(name="xt_bank", bufs=1))
-        bias_banks = stack.enter_context(tc.psum_pool(name="bias_banks", bufs=BIAS_AHEAD))
-        acc_banks = stack.enter_context(tc.psum_pool(name="acc_banks", bufs=2 * BANKS))
+        pairs = stack.enter_context(tc.tile_pool(name="pairs", bufs=2))
+        banks = stack.enter_context(tc.psum_pool(name="banks", bufs=8))
         stack.enter_context(tc.manual_schedule())
 
+        w_scales = keep.tile([P, COLS], U8, align_bytes=64)
+        nc.vector.memset(w_scales[:].bitcast(I32), 0)
         identity = keep.tile([P, P], F32)
         nc.vector.memset(identity[:], 0.0)
         make_identity(nc, identity[:], nomemset=True)
 
         cos_sin_bf = keep.tile([P, 2, HALF], BF16)
 
+        def load_table(queue, plane, table):
+            queue.dma_start(
+                out=cos_sin_bf[:, plane, :],
+                in_=table.unsqueeze(0).to_broadcast([BATCH, SEQ, HALF]),
+            )
+
+        load_table(nc.scalar, 0, cos)
         x_sb = keep.tile([P, DIM], BF16)
         nc.sync.dma_start(out=x_sb[:], in_=x_rows)
 
@@ -68,8 +76,6 @@ def tile_mla_pb_s_kernel(tc, x, wq_w_words, wq_w_scales, wq_b, cos, sin, out):
             out=b_sb[:], in_=wq_b.rearrange("(g p e) -> p g e", g=GROUPS, p=P)
         )
 
-        w_scales = keep.tile([P, COLS], U8, align_bytes=64)
-        nc.vector.memset(w_scales[:].bitcast(I32), 0)
         for r in range(4):
             nc.sync.dma_start(
                 out=w_scales[r:P:32, :].bitcast(I32),
@@ -77,21 +83,17 @@ def tile_mla_pb_s_kernel(tc, x, wq_w_words, wq_w_scales, wq_b, cos, sin, out):
             )
 
         w_words = keep.tile([P, 2 * COLS], U8, align_bytes=64)
-        for g in range(GROUPS):
-            group_bytes = slice(2 * GROUP_COLS * g, 2 * GROUP_COLS * (g + 1))
+        for half in range(2):
+            half_bytes = slice(COLS * half, COLS * (half + 1))
             nc.sync.dma_start(
-                out=w_words[:, group_bytes].bitcast(I32),
-                in_=w_rows[:, group_bytes].bitcast(I32),
+                out=w_words[:, half_bytes].bitcast(I32),
+                in_=w_rows[:, half_bytes].bitcast(I32),
             )
-
-        for plane, table in enumerate((cos, sin)):
-            nc.sync.dma_start(
-                out=cos_sin_bf[:, plane, :],
-                in_=table.unsqueeze(0).to_broadcast([BATCH, SEQ, HALF]),
-            )
+            if half == 0:
+                load_table(nc.sync, 1, sin)
 
         x_words = x_sb[:].bitcast(F32)
-        xt = xt_bank.tile([P, 2, P], F32)
+        xt = banks.tile([P, 2, P], F32, tag="bank")
         for u in range(2):
             nc.tensor.transpose(xt[:, u, :], x_words[:, u : DIM // 2 : 2], identity[:])
         x_grouped = keep.tile([P, P, 4], BF16, align_bytes=64)
@@ -107,7 +109,7 @@ def tile_mla_pb_s_kernel(tc, x, wq_w_words, wq_w_scales, wq_b, cos, sin, out):
         b_words = b_sb[:].bitcast(F32)
 
         def spread_bias(g):
-            spread = bias_banks.tile([P, WORD_PLANES, P], F32)
+            spread = banks.tile([P, WORD_PLANES, P], F32, tag="bank")
             for w in range(WORD_PLANES):
                 nc.tensor.transpose(
                     spread[:, w, :], b_words[:, g, w : w + 1].to_broadcast([P, P]), identity[:]
@@ -122,9 +124,9 @@ def tile_mla_pb_s_kernel(tc, x, wq_w_words, wq_w_scales, wq_b, cos, sin, out):
             )
             return bias
 
-        def multiply(g, bank):
-            first = GROUP_COLS * g + BANK_COLS * bank
-            acc = acc_banks.tile([P, BANK_HEADS, HEAD], F32)
+        def multiply(i):
+            first = BANK_COLS * i
+            acc = banks.tile([P, BANK_HEADS, HEAD], F32, tag="bank")
             acc_cols = acc[:].rearrange("p h d -> p (h d)")
             for offset, width in PASSES:
                 col = first + offset
@@ -139,69 +141,83 @@ def tile_mla_pb_s_kernel(tc, x, wq_w_words, wq_w_scales, wq_b, cos, sin, out):
                 )
             return acc
 
-        biases = [spread_bias(g) for g in range(BIAS_AHEAD)]
-
-        cos_cos = keep.tile([P, 2, HALF], F32)
+        biases = [spread_bias(0), spread_bias(1)]
+        cos_cos = keep.tile([P, HALF, 2], F32)
         nc.scalar.copy(
-            out=cos_cos[:], in_=cos_sin_bf[:, 0:1, :].to_broadcast([P, 2, HALF])
+            out=cos_cos[:], in_=cos_sin_bf[:, 0, :].unsqueeze(2).to_broadcast([P, HALF, 2])
         )
-        sin_sin = keep.tile([P, 2, HALF], F32)
-        nc.scalar.mul(out=sin_sin[:, 0, :], in_=cos_sin_bf[:, 1, :], mul=-1.0)
-        nc.scalar.copy(out=sin_sin[:, 1, :], in_=cos_sin_bf[:, 1, :])
-        planes_shape = [P, GROUP_HEADS, 2, HALF]
-        plane_shape = [P, GROUP_HEADS, HALF]
+        sin_sin = keep.tile([P, HALF, 2], F32)
+        nc.scalar.copy(out=sin_sin[:, :, 0], in_=cos_sin_bf[:, 1, :])
+        nc.scalar.mul(out=sin_sin[:, :, 1], in_=cos_sin_bf[:, 1, :], mul=-1.0)
+        accs = [multiply(i) for i in range(4)]
+        biases.append(spread_bias(2))
+        biases.append(spread_bias(3))
 
-        for g in range(GROUPS):
-            accs = [multiply(g, bank) for bank in range(BANKS)]
-            bias = biases[g]
-            bank_heads = [slice(BANK_HEADS * bank, BANK_HEADS * (bank + 1)) for bank in range(BANKS)]
+        rope_shape = [P, GROUP_HEADS, ROPE]
+        cos_all = cos_cos[:].rearrange("p j t -> p (j t)").unsqueeze(1).to_broadcast(rope_shape)
+        sin_all = sin_sin[:].rearrange("p j t -> p (j t)").unsqueeze(1).to_broadcast(rope_shape)
 
-            q = group.tile([P, GROUP_HEADS, HEAD], F32)
-            planes = group.tile([P, GROUP_HEADS, 2, HALF], F32)
-            for bank in range(BANKS):
-                nc.vector.tensor_tensor(
-                    out=planes[:, bank_heads[bank], :, :],
-                    in0=accs[bank][:, :, NOPE:HEAD].rearrange("p h (j t) -> p h t j", t=2),
-                    in1=bias[:, bank_heads[bank], NOPE:HEAD].rearrange("p h (j t) -> p h t j", t=2),
-                    op=ADD,
-                )
-            nc.scalar.copy(out=q[:, bank_heads[1], 0:NOPE], in_=accs[1][:, :, 0:NOPE])
-            if g + BIAS_AHEAD < GROUPS:
-                biases.append(spread_bias(g + BIAS_AHEAD))
+        qs = []
+
+        def add_bias(i, first=0, last=HEAD):
+            g, bank = divmod(i, BANKS)
+            if len(qs) == g:
+                q_new = group.tile([P, GROUP_HEADS, HEAD], F32, name="q")
+                qs.append(q_new)
+            heads = slice(BANK_HEADS * bank, BANK_HEADS * (bank + 1))
             nc.vector.tensor_tensor(
-                out=q[:, bank_heads[0], 0:NOPE],
-                in0=accs[0][:, :, 0:NOPE],
-                in1=bias[:, bank_heads[0], 0:NOPE],
+                out=qs[g][:, heads, first:last],
+                in0=accs[i][:, :, first:last],
+                in1=biases[g][:, heads, first:last],
                 op=ADD,
             )
-            nc.gpsimd.tensor_tensor(
-                out=q[:, bank_heads[1], 0:NOPE],
-                in0=q[:, bank_heads[1], 0:NOPE],
-                in1=bias[:, bank_heads[1], 0:NOPE],
-                op=ADD,
-            )
-            crossed = group.tile(planes_shape, F32)
-            for t in range(2):
-                nc.vector.tensor_tensor(
-                    out=crossed[:, :, t, :],
-                    in0=planes[:, :, 1 - t, :],
-                    in1=sin_sin[:, t : t + 1, :].to_broadcast(plane_shape),
-                    op=MULT,
-                )
-            straight = group.tile(planes_shape, F32)
+
+        pair_view = "p h (j t) -> p h j t"
+        products = {}
+
+        def multiply_tables(g):
+            straight = pairs.tile(rope_shape, F32, name="straight")
             nc.vector.tensor_tensor(
-                out=straight[:],
-                in0=planes[:],
-                in1=cos_cos[:].unsqueeze(1).to_broadcast(planes_shape),
-                op=MULT,
+                out=straight[:], in0=qs[g][:, :, NOPE:HEAD], in1=cos_all, op=MULT
             )
+            crossed = pairs.tile(rope_shape, F32, name="crossed")
             nc.vector.tensor_tensor(
-                out=q[:, :, NOPE:HEAD].rearrange("p h (j t) -> p h j t", t=2),
-                in0=straight[:].rearrange("p h t j -> p h j t"),
-                in1=crossed[:].rearrange("p h t j -> p h j t"),
+                out=crossed[:], in0=qs[g][:, :, NOPE:HEAD], in1=sin_all, op=MULT
+            )
+            products[g] = (straight, crossed)
+
+        def finish(g, engine):
+            straight, crossed = products[g]
+            engine.tensor_tensor(
+                out=qs[g][:, :, NOPE:HEAD].rearrange(pair_view, t=2),
+                in0=straight[:].rearrange(pair_view, t=2),
+                in1=crossed[:].rearrange(pair_view, t=2)[:, :, :, ::-1],
                 op=ADD,
             )
             nc.sync.dma_start(
                 out=out_rows[:, GROUP_COLS * g : GROUP_COLS * (g + 1)],
-                in_=q[:].rearrange("p h d -> p (h d)"),
+                in_=qs[g][:].rearrange("p h d -> p (h d)"),
             )
+
+        add_bias(0)
+        add_bias(1)
+        accs.append(multiply(4))
+        accs.append(multiply(5))
+        accs.append(multiply(6))
+        accs.append(multiply(7))
+        add_bias(2)
+        multiply_tables(0)
+        finish(0, nc.gpsimd)
+        add_bias(3)
+        add_bias(4)
+        multiply_tables(1)
+        finish(1, nc.gpsimd)
+        add_bias(5)
+        add_bias(6, NOPE, HEAD)
+        add_bias(7, NOPE, HEAD)
+        multiply_tables(2)
+        finish(2, nc.gpsimd)
+        add_bias(6, 0, NOPE)
+        add_bias(7, 0, NOPE)
+        multiply_tables(3)
+        finish(3, nc.vector)

@@ -92,6 +92,11 @@ def tile_mla_pb_s_kernel(tc, x, wq_w_words, wq_w_scales, wq_b, cos, sin, out):
             if half == 0:
                 load_table(nc.sync, 1, sin)
 
+        tables = keep.tile([P, 2, HALF, 2], F32)
+        nc.scalar.copy(
+            out=tables[:, 0, :, :], in_=cos_sin_bf[:, 0, :].unsqueeze(2).to_broadcast([P, HALF, 2])
+        )
+
         x_words = x_sb[:].bitcast(F32)
         xt = banks.tile([P, 2, P], F32, tag="bank")
         for u in range(2):
@@ -124,14 +129,12 @@ def tile_mla_pb_s_kernel(tc, x, wq_w_words, wq_w_scales, wq_b, cos, sin, out):
             )
             return bias
 
-        def multiply(i):
-            first = BANK_COLS * i
-            acc = banks.tile([P, BANK_HEADS, HEAD], F32, tag="bank")
-            acc_cols = acc[:].rearrange("p h d -> p (h d)")
-            for offset, width in PASSES:
-                col = first + offset
+        def multiply(g, first, width):
+            acc = banks.tile([P, GROUP_HEADS, width], F32, tag="bank")
+            for h in range(GROUP_HEADS):
+                col = GROUP_COLS * g + HEAD * h + first
                 nc.tensor.matmul_mx(
-                    out=acc_cols[:, offset : offset + width],
+                    out=acc[:, h, :],
                     lhsT=x_codes[:].bitcast(FP8X4),
                     lhsT_scale=x_scales[:],
                     rhs=w_words[:, 2 * col : 2 * (col + width)].bitcast(FP4X4),
@@ -141,83 +144,80 @@ def tile_mla_pb_s_kernel(tc, x, wq_w_words, wq_w_scales, wq_b, cos, sin, out):
                 )
             return acc
 
-        biases = [spread_bias(0), spread_bias(1)]
-        cos_cos = keep.tile([P, HALF, 2], F32)
-        nc.scalar.copy(
-            out=cos_cos[:], in_=cos_sin_bf[:, 0, :].unsqueeze(2).to_broadcast([P, HALF, 2])
-        )
-        sin_sin = keep.tile([P, HALF, 2], F32)
-        nc.scalar.copy(out=sin_sin[:, :, 0], in_=cos_sin_bf[:, 1, :])
-        nc.scalar.mul(out=sin_sin[:, :, 1], in_=cos_sin_bf[:, 1, :], mul=-1.0)
-        accs = [multiply(i) for i in range(4)]
-        biases.append(spread_bias(2))
+        rotated_acc = {}
+        plain_acc = {}
+
+        def multiply_rotated(g):
+            rotated_acc[g] = multiply(g, NOPE, ROPE)
+
+        def multiply_plain(g):
+            plain_acc[g] = multiply(g, 0, NOPE)
+
+        biases = [spread_bias(0), spread_bias(1), spread_bias(2)]
+        nc.scalar.copy(out=tables[:, 1, :, 0], in_=cos_sin_bf[:, 1, :])
+        nc.scalar.mul(out=tables[:, 1, :, 1], in_=cos_sin_bf[:, 1, :], mul=-1.0)
+        multiply_rotated(0)
+        multiply_rotated(1)
+        multiply_plain(0)
         biases.append(spread_bias(3))
+        multiply_rotated(2)
+        multiply_plain(1)
 
-        rope_shape = [P, GROUP_HEADS, ROPE]
-        cos_all = cos_cos[:].rearrange("p j t -> p (j t)").unsqueeze(1).to_broadcast(rope_shape)
-        sin_all = sin_sin[:].rearrange("p j t -> p (j t)").unsqueeze(1).to_broadcast(rope_shape)
-
-        qs = []
-
-        def add_bias(i, first=0, last=HEAD):
-            g, bank = divmod(i, BANKS)
-            if len(qs) == g:
-                q_new = group.tile([P, GROUP_HEADS, HEAD], F32, name="q")
-                qs.append(q_new)
-            heads = slice(BANK_HEADS * bank, BANK_HEADS * (bank + 1))
-            nc.vector.tensor_tensor(
-                out=qs[g][:, heads, first:last],
-                in0=accs[i][:, :, first:last],
-                in1=biases[g][:, heads, first:last],
-                op=ADD,
-            )
-
+        products_shape = [P, GROUP_HEADS, 2, ROPE]
         pair_view = "p h (j t) -> p h j t"
+        qs = [group.tile([P, GROUP_HEADS, HEAD], F32, name="q") for g in range(GROUPS)]
         products = {}
 
-        def multiply_tables(g):
-            straight = pairs.tile(rope_shape, F32, name="straight")
+        def add_rotated(g):
             nc.vector.tensor_tensor(
-                out=straight[:], in0=qs[g][:, :, NOPE:HEAD], in1=cos_all, op=MULT
-            )
-            crossed = pairs.tile(rope_shape, F32, name="crossed")
-            nc.vector.tensor_tensor(
-                out=crossed[:], in0=qs[g][:, :, NOPE:HEAD], in1=sin_all, op=MULT
-            )
-            products[g] = (straight, crossed)
-
-        def finish(g, engine):
-            straight, crossed = products[g]
-            engine.tensor_tensor(
-                out=qs[g][:, :, NOPE:HEAD].rearrange(pair_view, t=2),
-                in0=straight[:].rearrange(pair_view, t=2),
-                in1=crossed[:].rearrange(pair_view, t=2)[:, :, :, ::-1],
+                out=qs[g][:, :, NOPE:HEAD],
+                in0=rotated_acc[g][:],
+                in1=biases[g][:, :, NOPE:HEAD],
                 op=ADD,
             )
+
+        def add_plain(g):
+            nc.vector.tensor_tensor(
+                out=qs[g][:, :, 0:NOPE],
+                in0=plain_acc[g][:],
+                in1=biases[g][:, :, 0:NOPE],
+                op=ADD,
+            )
+
+        def multiply_tables(g):
+            both = pairs.tile(products_shape, F32, name="both")
+            nc.vector.tensor_tensor(
+                out=both[:],
+                in0=qs[g][:, :, NOPE:HEAD].unsqueeze(2).to_broadcast(products_shape),
+                in1=tables[:].rearrange("p w j t -> p w (j t)").unsqueeze(1).to_broadcast(products_shape),
+                op=MULT,
+            )
+            products[g] = both
+
+        def finish_sum(g):
+            nc.gpsimd.tensor_tensor(
+                out=qs[g][:, :, NOPE:HEAD].rearrange(pair_view, t=2),
+                in0=products[g][:, :, 0, :].rearrange(pair_view, t=2),
+                in1=products[g][:, :, 1, :].rearrange(pair_view, t=2)[:, :, :, ::-1],
+                op=ADD,
+            )
+
+        def store(g):
             nc.sync.dma_start(
                 out=out_rows[:, GROUP_COLS * g : GROUP_COLS * (g + 1)],
                 in_=qs[g][:].rearrange("p h d -> p (h d)"),
             )
 
-        add_bias(0)
-        add_bias(1)
-        accs.append(multiply(4))
-        accs.append(multiply(5))
-        accs.append(multiply(6))
-        accs.append(multiply(7))
-        add_bias(2)
-        multiply_tables(0)
-        finish(0, nc.gpsimd)
-        add_bias(3)
-        add_bias(4)
-        multiply_tables(1)
-        finish(1, nc.gpsimd)
-        add_bias(5)
-        add_bias(6, NOPE, HEAD)
-        add_bias(7, NOPE, HEAD)
-        multiply_tables(2)
-        finish(2, nc.gpsimd)
-        add_bias(6, 0, NOPE)
-        add_bias(7, 0, NOPE)
-        multiply_tables(3)
-        finish(3, nc.vector)
+        add_rotated(0)
+        add_rotated(1)
+        for g in range(GROUPS):
+            multiply_tables(g)
+            finish_sum(g)
+            add_plain(g)
+            if g + 2 < GROUPS:
+                add_rotated(g + 2)
+            if g == 0:
+                multiply_rotated(3)
+                multiply_plain(2)
+                multiply_plain(3)
+            store(g)

@@ -36,6 +36,8 @@ WORD_PLANES = GROUP_WORDS // P
 
 BIAS_AHEAD = 2
 
+WARM_PASSES = 4
+
 FLOPS = 2 * P * DIM * COLS
 
 
@@ -52,6 +54,12 @@ def tile_mla_pb_s_kernel(tc, x, wq_w_words, wq_w_scales, wq_b, cos, sin, out):
         pairs = stack.enter_context(tc.tile_pool(name="pairs", bufs=2))
         banks = stack.enter_context(tc.psum_pool(name="banks", bufs=8))
         stack.enter_context(tc.manual_schedule())
+
+        zeros = keep.tile([P, P], F32)
+        nc.gpsimd.memset(zeros[:], 0.0)
+        warm = banks.tile([P, P], F32, tag="bank")
+        for i in range(WARM_PASSES):
+            nc.tensor.matmul(out=warm[:], lhsT=zeros[:], rhs=zeros[:], start=True, stop=True)
 
         w_scales = keep.tile([P, COLS], U8, align_bytes=64)
         nc.vector.memset(w_scales[:].bitcast(I32), 0)
@@ -176,11 +184,11 @@ def tile_mla_pb_s_kernel(tc, x, wq_w_words, wq_w_scales, wq_b, cos, sin, out):
                 op=ADD,
             )
 
-        def add_plain(g):
+        def add_plain(g, heads):
             nc.vector.tensor_tensor(
-                out=qs[g][:, :, 0:NOPE],
-                in0=plain_acc[g][:],
-                in1=biases[g][:, :, 0:NOPE],
+                out=qs[g][:, heads, 0:NOPE],
+                in0=plain_acc[g][:, heads, :],
+                in1=biases[g][:, heads, 0:NOPE],
                 op=ADD,
             )
 
@@ -194,30 +202,36 @@ def tile_mla_pb_s_kernel(tc, x, wq_w_words, wq_w_scales, wq_b, cos, sin, out):
             )
             products[g] = both
 
-        def finish_sum(g):
+        def finish_sum(g, heads):
             nc.gpsimd.tensor_tensor(
-                out=qs[g][:, :, NOPE:HEAD].rearrange(pair_view, t=2),
-                in0=products[g][:, :, 0, :].rearrange(pair_view, t=2),
-                in1=products[g][:, :, 1, :].rearrange(pair_view, t=2)[:, :, :, ::-1],
+                out=qs[g][:, heads, NOPE:HEAD].rearrange(pair_view, t=2),
+                in0=products[g][:, heads, 0, :].rearrange(pair_view, t=2),
+                in1=products[g][:, heads, 1, :].rearrange(pair_view, t=2)[:, :, :, ::-1],
                 op=ADD,
             )
 
-        def store(g):
+        def store(g, heads):
+            first = GROUP_COLS * g + HEAD * heads.start
             nc.sync.dma_start(
-                out=out_rows[:, GROUP_COLS * g : GROUP_COLS * (g + 1)],
-                in_=qs[g][:].rearrange("p h d -> p (h d)"),
+                out=out_rows[:, first : first + HEAD * (heads.stop - heads.start)],
+                in_=qs[g][:, heads, :].rearrange("p h d -> p (h d)"),
             )
 
         add_rotated(0)
         add_rotated(1)
+        whole = (slice(0, GROUP_HEADS),)
+        halves = (slice(0, GROUP_HEADS // 2), slice(GROUP_HEADS // 2, GROUP_HEADS))
         for g in range(GROUPS):
             multiply_tables(g)
-            finish_sum(g)
-            add_plain(g)
+            pieces = halves if g == GROUPS - 1 else whole
+            for heads in pieces:
+                finish_sum(g, heads)
+                add_plain(g, heads)
             if g + 2 < GROUPS:
                 add_rotated(g + 2)
             if g == 0:
                 multiply_rotated(3)
                 multiply_plain(2)
                 multiply_plain(3)
-            store(g)
+            for heads in pieces:
+                store(g, heads)

@@ -52,7 +52,8 @@ def tile_mla_pb_s_kernel(tc, x, wq_w_words, wq_w_scales, wq_b, cos, sin, out):
         keep = stack.enter_context(tc.tile_pool(name="keep", bufs=1))
         group = stack.enter_context(tc.tile_pool(name="group", bufs=GROUPS))
         pairs = stack.enter_context(tc.tile_pool(name="pairs", bufs=2))
-        banks = stack.enter_context(tc.psum_pool(name="banks", bufs=8))
+        banks = stack.enter_context(tc.psum_pool(name="banks", bufs=7))
+        table_bank = stack.enter_context(tc.psum_pool(name="table_bank", bufs=1))
         stack.enter_context(tc.manual_schedule())
 
         zeros = keep.tile([P, P], F32)
@@ -167,6 +168,14 @@ def tile_mla_pb_s_kernel(tc, x, wq_w_words, wq_w_scales, wq_b, cos, sin, out):
         multiply_rotated(0)
         multiply_rotated(1)
         multiply_plain(0)
+        tables_ps = table_bank.tile([P, 2, ROPE], F32)
+        nc.tensor.matmul(
+            out=tables_ps[:].rearrange("p w c -> p (w c)"),
+            lhsT=identity[:],
+            rhs=tables[:].rearrange("p w j t -> p (w j t)"),
+            start=True,
+            stop=True,
+        )
         biases.append(spread_bias(3))
         multiply_rotated(2)
         multiply_plain(1)
@@ -197,13 +206,13 @@ def tile_mla_pb_s_kernel(tc, x, wq_w_words, wq_w_scales, wq_b, cos, sin, out):
             nc.vector.tensor_tensor(
                 out=both[:],
                 in0=qs[g][:, :, NOPE:HEAD].unsqueeze(2).to_broadcast(products_shape),
-                in1=tables[:].rearrange("p w j t -> p w (j t)").unsqueeze(1).to_broadcast(products_shape),
+                in1=tables_ps[:].unsqueeze(1).to_broadcast(products_shape),
                 op=MULT,
             )
             products[g] = both
 
-        def finish_sum(g, heads):
-            nc.gpsimd.tensor_tensor(
+        def finish_sum(engine, g, heads):
+            engine.tensor_tensor(
                 out=qs[g][:, heads, NOPE:HEAD].rearrange(pair_view, t=2),
                 in0=products[g][:, heads, 0, :].rearrange(pair_view, t=2),
                 in1=products[g][:, heads, 1, :].rearrange(pair_view, t=2)[:, :, :, ::-1],
@@ -217,21 +226,31 @@ def tile_mla_pb_s_kernel(tc, x, wq_w_words, wq_w_scales, wq_b, cos, sin, out):
                 in_=qs[g][:, heads, :].rearrange("p h d -> p (h d)"),
             )
 
+        whole = slice(0, GROUP_HEADS)
+        halves = (slice(0, GROUP_HEADS // 2), slice(GROUP_HEADS // 2, GROUP_HEADS))
         add_rotated(0)
         add_rotated(1)
-        whole = (slice(0, GROUP_HEADS),)
-        halves = (slice(0, GROUP_HEADS // 2), slice(GROUP_HEADS // 2, GROUP_HEADS))
-        for g in range(GROUPS):
-            multiply_tables(g)
-            pieces = halves if g == GROUPS - 1 else whole
-            for heads in pieces:
-                finish_sum(g, heads)
-                add_plain(g, heads)
-            if g + 2 < GROUPS:
-                add_rotated(g + 2)
-            if g == 0:
-                multiply_rotated(3)
-                multiply_plain(2)
-                multiply_plain(3)
-            for heads in pieces:
-                store(g, heads)
+        add_plain(0, whole)
+        multiply_tables(0)
+        finish_sum(nc.gpsimd, 0, whole)
+        store(0, whole)
+        multiply_rotated(3)
+        multiply_plain(2)
+        multiply_plain(3)
+        add_rotated(2)
+        multiply_tables(1)
+        finish_sum(nc.gpsimd, 1, whole)
+        add_plain(1, whole)
+        store(1, whole)
+        add_rotated(3)
+        multiply_tables(2)
+        finish_sum(nc.gpsimd, 2, whole)
+        add_plain(2, whole)
+        store(2, whole)
+        multiply_tables(3)
+        finish_sum(nc.gpsimd, 3, halves[0])
+        add_plain(3, halves[0])
+        add_plain(3, halves[1])
+        finish_sum(nc.vector, 3, halves[1])
+        store(3, halves[0])
+        store(3, halves[1])

@@ -37,6 +37,7 @@ WORD_PLANES = GROUP_WORDS // P
 BIAS_AHEAD = 2
 
 WARM_PASSES = 4
+TURNED = 1
 
 FLOPS = 2 * P * DIM * COLS
 
@@ -51,7 +52,7 @@ def tile_mla_pb_s_kernel(tc, x, wq_w_words, wq_w_scales, wq_b, cos, sin, out):
     with ExitStack() as stack:
         keep = stack.enter_context(tc.tile_pool(name="keep", bufs=1))
         group = stack.enter_context(tc.tile_pool(name="group", bufs=GROUPS))
-        pairs = stack.enter_context(tc.tile_pool(name="pairs", bufs=2))
+        pairs = stack.enter_context(tc.tile_pool(name="pairs", bufs=GROUPS))
         banks = stack.enter_context(tc.psum_pool(name="banks", bufs=7))
         table_bank = stack.enter_context(tc.psum_pool(name="table_bank", bufs=1))
         stack.enter_context(tc.manual_schedule())
@@ -100,6 +101,15 @@ def tile_mla_pb_s_kernel(tc, x, wq_w_words, wq_w_scales, wq_b, cos, sin, out):
             )
             if half == 0:
                 load_table(nc.sync, 1, sin)
+
+        b_col = keep.tile([P, GROUP_HEADS, 2], BF16)
+        with nc.allow_non_contiguous_dma(reason="one bias entry to a partition"):
+            nc.sync.dma_start(
+                out=b_col[:, :, 0:1],
+                in_=wq_b.rearrange("(h d) -> d h", d=HEAD)[
+                    0:NOPE, GROUP_HEADS * TURNED : GROUP_HEADS * (TURNED + 1)
+                ].unsqueeze(2),
+            )
 
         tables = keep.tile([P, 2, HALF, 2], F32)
         nc.scalar.copy(
@@ -176,9 +186,35 @@ def tile_mla_pb_s_kernel(tc, x, wq_w_words, wq_w_scales, wq_b, cos, sin, out):
             start=True,
             stop=True,
         )
-        biases.append(spread_bias(3))
+        turned = banks.tile([P, GROUP_HEADS, P], F32, tag="bank")
+        for h in range(GROUP_HEADS):
+            col = GROUP_COLS * TURNED + HEAD * h
+            nc.tensor.matmul_mx(
+                out=turned[:, h, :],
+                lhsT=w_words[:, 2 * col : 2 * (col + NOPE)].bitcast(FP4X4),
+                lhsT_scale=w_scales[:, col : col + NOPE],
+                rhs=x_codes[:].bitcast(FP8X4),
+                rhs_scale=x_scales[:],
+                start=True,
+                stop=True,
+            )
+        turned_sb = keep.tile([P, GROUP_HEADS, P], F32)
+        for h in range(GROUP_HEADS):
+            nc.scalar.activation(
+                out=turned_sb[:, h, :],
+                in_=turned[:, h, :],
+                func=mybir.ActivationFunctionType.Identity,
+                bias=b_col[:, h, 0:1],
+                scale=1.0,
+            )
         multiply_rotated(2)
-        multiply_plain(1)
+        multiply_plain(2)
+        biases.append(spread_bias(3))
+        turned_back = banks.tile([P, GROUP_HEADS, NOPE], F32, tag="bank")
+        for h in range(GROUP_HEADS):
+            nc.tensor.transpose(turned_back[:, h, :], turned_sb[:, h, :], identity[:])
+        multiply_rotated(3)
+        multiply_plain(3)
 
         products_shape = [P, GROUP_HEADS, 2, ROPE]
         pair_view = "p h (j t) -> p h j t"
@@ -201,12 +237,12 @@ def tile_mla_pb_s_kernel(tc, x, wq_w_words, wq_w_scales, wq_b, cos, sin, out):
                 op=ADD,
             )
 
-        def multiply_tables(g):
+        def multiply_tables(engine, both_tables, g):
             both = pairs.tile(products_shape, F32, name="both")
-            nc.vector.tensor_tensor(
+            engine.tensor_tensor(
                 out=both[:],
                 in0=qs[g][:, :, NOPE:HEAD].unsqueeze(2).to_broadcast(products_shape),
-                in1=tables_ps[:].unsqueeze(1).to_broadcast(products_shape),
+                in1=both_tables.unsqueeze(1).to_broadcast(products_shape),
                 op=MULT,
             )
             products[g] = both
@@ -230,24 +266,21 @@ def tile_mla_pb_s_kernel(tc, x, wq_w_words, wq_w_scales, wq_b, cos, sin, out):
         halves = (slice(0, GROUP_HEADS // 2), slice(GROUP_HEADS // 2, GROUP_HEADS))
         add_rotated(0)
         add_rotated(1)
+        multiply_tables(nc.gpsimd, tables[:].rearrange("p w j t -> p w (j t)"), 1)
         add_plain(0, whole)
-        multiply_tables(0)
+        multiply_tables(nc.vector, tables_ps[:], 0)
         finish_sum(nc.gpsimd, 0, whole)
         store(0, whole)
-        multiply_rotated(3)
-        multiply_plain(2)
-        multiply_plain(3)
-        add_rotated(2)
-        multiply_tables(1)
+        nc.scalar.copy(out=qs[TURNED][:, :, 0:NOPE], in_=turned_back[:])
         finish_sum(nc.gpsimd, 1, whole)
-        add_plain(1, whole)
         store(1, whole)
-        add_rotated(3)
-        multiply_tables(2)
+        add_rotated(2)
+        multiply_tables(nc.vector, tables_ps[:], 2)
         finish_sum(nc.gpsimd, 2, whole)
         add_plain(2, whole)
         store(2, whole)
-        multiply_tables(3)
+        add_rotated(3)
+        multiply_tables(nc.vector, tables_ps[:], 3)
         finish_sum(nc.gpsimd, 3, halves[0])
         add_plain(3, halves[0])
         add_plain(3, halves[1])

@@ -52,7 +52,6 @@ def tile_mla_pb_s_kernel(tc, x, wq_w_words, wq_w_scales, wq_b, cos, sin, out):
     with ExitStack() as stack:
         keep = stack.enter_context(tc.tile_pool(name="keep", bufs=1))
         group = stack.enter_context(tc.tile_pool(name="group", bufs=GROUPS))
-        pairs = stack.enter_context(tc.tile_pool(name="pairs", bufs=GROUPS))
         banks = stack.enter_context(tc.psum_pool(name="banks", bufs=7))
         table_bank = stack.enter_context(tc.psum_pool(name="table_bank", bufs=1))
         stack.enter_context(tc.manual_schedule())
@@ -92,6 +91,7 @@ def tile_mla_pb_s_kernel(tc, x, wq_w_words, wq_w_scales, wq_b, cos, sin, out):
                 in_=scale_rows[r:16:4, :].bitcast(I32),
             )
 
+        b_col = keep.tile([P, GROUP_HEADS, 2], BF16)
         w_words = keep.tile([P, 2 * COLS], U8, align_bytes=64)
         for half in range(2):
             half_bytes = slice(COLS * half, COLS * (half + 1))
@@ -101,15 +101,13 @@ def tile_mla_pb_s_kernel(tc, x, wq_w_words, wq_w_scales, wq_b, cos, sin, out):
             )
             if half == 0:
                 load_table(nc.sync, 1, sin)
-
-        b_col = keep.tile([P, GROUP_HEADS, 2], BF16)
-        with nc.allow_non_contiguous_dma(reason="one bias entry to a partition"):
-            nc.sync.dma_start(
-                out=b_col[:, :, 0:1],
-                in_=wq_b.rearrange("(h d) -> d h", d=HEAD)[
-                    0:NOPE, GROUP_HEADS * TURNED : GROUP_HEADS * (TURNED + 1)
-                ].unsqueeze(2),
-            )
+                with nc.allow_non_contiguous_dma(reason="one bias entry to a partition"):
+                    nc.sync.dma_start(
+                        out=b_col[:, :, 0:1],
+                        in_=wq_b.rearrange("(h d) -> d h", d=HEAD)[
+                            0:NOPE, GROUP_HEADS * TURNED : GROUP_HEADS * (TURNED + 1)
+                        ].unsqueeze(2),
+                    )
 
         tables = keep.tile([P, 2, HALF, 2], F32)
         nc.scalar.copy(
@@ -148,36 +146,37 @@ def tile_mla_pb_s_kernel(tc, x, wq_w_words, wq_w_scales, wq_b, cos, sin, out):
             )
             return bias
 
-        def multiply(g, first, width):
-            acc = banks.tile([P, GROUP_HEADS, width], F32, tag="bank")
-            for h in range(GROUP_HEADS):
-                col = GROUP_COLS * g + HEAD * h + first
-                nc.tensor.matmul_mx(
-                    out=acc[:, h, :],
-                    lhsT=x_codes[:].bitcast(FP8X4),
-                    lhsT_scale=x_scales[:],
-                    rhs=w_words[:, 2 * col : 2 * (col + width)].bitcast(FP4X4),
-                    rhs_scale=w_scales[:, col : col + width],
-                    start=True,
-                    stop=True,
-                )
-            return acc
+        def x_times_w(acc_cols, col, width):
+            nc.tensor.matmul_mx(
+                out=acc_cols,
+                lhsT=x_codes[:].bitcast(FP8X4),
+                lhsT_scale=x_scales[:],
+                rhs=w_words[:, 2 * col : 2 * (col + width)].bitcast(FP4X4),
+                rhs_scale=w_scales[:, col : col + width],
+                start=True,
+                stop=True,
+            )
 
-        rotated_acc = {}
-        plain_acc = {}
+        accs = {}
 
-        def multiply_rotated(g):
-            rotated_acc[g] = multiply(g, NOPE, ROPE)
-
-        def multiply_plain(g):
-            plain_acc[g] = multiply(g, 0, NOPE)
+        def multiply(i):
+            acc = banks.tile([P, BANK_HEADS, HEAD], F32, tag="bank")
+            acc_cols = acc[:].rearrange("p h d -> p (h d)")
+            for offset, width in PASSES:
+                x_times_w(acc_cols[:, offset : offset + width], BANK_COLS * i + offset, width)
+            accs[i] = acc
 
         biases = [spread_bias(0), spread_bias(1), spread_bias(2)]
         nc.scalar.copy(out=tables[:, 1, :, 0], in_=cos_sin_bf[:, 1, :])
         nc.scalar.mul(out=tables[:, 1, :, 1], in_=cos_sin_bf[:, 1, :], mul=-1.0)
-        multiply_rotated(0)
-        multiply_rotated(1)
-        multiply_plain(0)
+
+        multiply(0)
+        multiply(1)
+        window = 2 * ROPE + NOPE
+        turned_rope = banks.tile([P, BANKS, window], F32, tag="bank")
+        for k in range(BANKS):
+            x_times_w(turned_rope[:, k, :], GROUP_COLS * TURNED + BANK_COLS * k + NOPE, window)
+        biases.append(spread_bias(3))
         tables_ps = table_bank.tile([P, 2, ROPE], F32)
         nc.tensor.matmul(
             out=tables_ps[:].rearrange("p w c -> p (w c)"),
@@ -207,45 +206,44 @@ def tile_mla_pb_s_kernel(tc, x, wq_w_words, wq_w_scales, wq_b, cos, sin, out):
                 bias=b_col[:, h, 0:1],
                 scale=1.0,
             )
-        multiply_rotated(2)
-        multiply_plain(2)
-        biases.append(spread_bias(3))
+        for i in (4, 5, 6, 7):
+            multiply(i)
         turned_back = banks.tile([P, GROUP_HEADS, NOPE], F32, tag="bank")
         for h in range(GROUP_HEADS):
             nc.tensor.transpose(turned_back[:, h, :], turned_sb[:, h, :], identity[:])
-        multiply_rotated(3)
-        multiply_plain(3)
 
-        products_shape = [P, GROUP_HEADS, 2, ROPE]
         pair_view = "p h (j t) -> p h j t"
         qs = [group.tile([P, GROUP_HEADS, HEAD], F32, name="q") for g in range(GROUPS)]
-        products = {}
+        products = [group.tile([P, GROUP_HEADS, 2, ROPE], F32, name="both") for g in range(GROUPS)]
+        whole = slice(0, GROUP_HEADS)
+        halves = (slice(0, BANK_HEADS), slice(BANK_HEADS, GROUP_HEADS))
 
-        def add_rotated(g):
+        def add_bias(i, first=0, last=HEAD):
+            g, bank = divmod(i, BANKS)
             nc.vector.tensor_tensor(
-                out=qs[g][:, :, NOPE:HEAD],
-                in0=rotated_acc[g][:],
-                in1=biases[g][:, :, NOPE:HEAD],
+                out=qs[g][:, halves[bank], first:last],
+                in0=accs[i][:, :, first:last],
+                in1=biases[g][:, halves[bank], first:last],
                 op=ADD,
             )
 
-        def add_plain(g, heads):
+        def add_bias_turned():
+            ends = "p (k s) c -> p k s c"
             nc.vector.tensor_tensor(
-                out=qs[g][:, heads, 0:NOPE],
-                in0=plain_acc[g][:, heads, :],
-                in1=biases[g][:, heads, 0:NOPE],
+                out=qs[TURNED][:, :, NOPE:HEAD].rearrange(ends, s=2),
+                in0=turned_rope[:].rearrange("p k (s c) -> p k s c", c=ROPE)[:, :, 0:4:3, :],
+                in1=biases[TURNED][:, :, NOPE:HEAD].rearrange(ends, s=2),
                 op=ADD,
             )
 
-        def multiply_tables(engine, both_tables, g):
-            both = pairs.tile(products_shape, F32, name="both")
+        def multiply_tables(engine, both_tables, g, heads):
+            shape = [P, heads.stop - heads.start, 2, ROPE]
             engine.tensor_tensor(
-                out=both[:],
-                in0=qs[g][:, :, NOPE:HEAD].unsqueeze(2).to_broadcast(products_shape),
-                in1=both_tables.unsqueeze(1).to_broadcast(products_shape),
+                out=products[g][:, heads, :, :],
+                in0=qs[g][:, heads, NOPE:HEAD].unsqueeze(2).to_broadcast(shape),
+                in1=both_tables.unsqueeze(1).to_broadcast(shape),
                 op=MULT,
             )
-            products[g] = both
 
         def finish_sum(engine, g, heads):
             engine.tensor_tensor(
@@ -262,28 +260,27 @@ def tile_mla_pb_s_kernel(tc, x, wq_w_words, wq_w_scales, wq_b, cos, sin, out):
                 in_=qs[g][:, heads, :].rearrange("p h d -> p (h d)"),
             )
 
-        whole = slice(0, GROUP_HEADS)
-        halves = (slice(0, GROUP_HEADS // 2), slice(GROUP_HEADS // 2, GROUP_HEADS))
-        add_rotated(0)
-        add_rotated(1)
-        multiply_tables(nc.gpsimd, tables[:].rearrange("p w j t -> p w (j t)"), 1)
-        add_plain(0, whole)
-        multiply_tables(nc.vector, tables_ps[:], 0)
+        add_bias(0)
+        add_bias(1)
+        add_bias_turned()
+        multiply_tables(nc.vector, tables_ps[:], 0, whole)
         finish_sum(nc.gpsimd, 0, whole)
         store(0, whole)
+        multiply_tables(nc.vector, tables_ps[:], TURNED, whole)
         nc.scalar.copy(out=qs[TURNED][:, :, 0:NOPE], in_=turned_back[:])
-        finish_sum(nc.gpsimd, 1, whole)
-        store(1, whole)
-        add_rotated(2)
-        multiply_tables(nc.vector, tables_ps[:], 2)
+        finish_sum(nc.gpsimd, TURNED, whole)
+        store(TURNED, whole)
+        add_bias(4)
+        add_bias(5)
+        add_bias(6, NOPE, HEAD)
+        multiply_tables(nc.vector, tables_ps[:], 2, whole)
         finish_sum(nc.gpsimd, 2, whole)
-        add_plain(2, whole)
         store(2, whole)
-        add_rotated(3)
-        multiply_tables(nc.vector, tables_ps[:], 3)
+        add_bias(7, NOPE, HEAD)
+        add_bias(6, 0, NOPE)
+        multiply_tables(nc.vector, tables_ps[:], 3, whole)
         finish_sum(nc.gpsimd, 3, halves[0])
-        add_plain(3, halves[0])
-        add_plain(3, halves[1])
+        add_bias(7, 0, NOPE)
         finish_sum(nc.vector, 3, halves[1])
         store(3, halves[0])
         store(3, halves[1])

@@ -37,7 +37,7 @@ WORD_PLANES = GROUP_WORDS // P
 BIAS_AHEAD = 2
 
 WARM_PASSES = 4
-TURNED = 1
+TURNED = (1, 2)
 
 FLOPS = 2 * P * DIM * COLS
 
@@ -91,7 +91,7 @@ def tile_mla_pb_s_kernel(tc, x, wq_w_words, wq_w_scales, wq_b, cos, sin, out):
                 in_=scale_rows[r:16:4, :].bitcast(I32),
             )
 
-        b_col = keep.tile([P, GROUP_HEADS, 2], BF16)
+        b_col = keep.tile([P, len(TURNED) * GROUP_HEADS, 2], BF16)
         w_words = keep.tile([P, 2 * COLS], U8, align_bytes=64)
         for half in range(2):
             half_bytes = slice(COLS * half, COLS * (half + 1))
@@ -105,7 +105,7 @@ def tile_mla_pb_s_kernel(tc, x, wq_w_words, wq_w_scales, wq_b, cos, sin, out):
                     nc.sync.dma_start(
                         out=b_col[:, :, 0:1],
                         in_=wq_b.rearrange("(h d) -> d h", d=HEAD)[
-                            0:NOPE, GROUP_HEADS * TURNED : GROUP_HEADS * (TURNED + 1)
+                            0:NOPE, GROUP_HEADS * TURNED[0] : GROUP_HEADS * (TURNED[-1] + 1)
                         ].unsqueeze(2),
                     )
 
@@ -170,12 +170,55 @@ def tile_mla_pb_s_kernel(tc, x, wq_w_words, wq_w_scales, wq_b, cos, sin, out):
         nc.scalar.copy(out=tables[:, 1, :, 0], in_=cos_sin_bf[:, 1, :])
         nc.scalar.mul(out=tables[:, 1, :, 1], in_=cos_sin_bf[:, 1, :], mul=-1.0)
 
+        window = 2 * ROPE + NOPE
+        turned_rope = {}
+        turned = {}
+        turned_sb = {}
+        turned_back = {}
+
+        def multiply_turned_rotated(g):
+            rope_bank = banks.tile([P, BANKS, window], F32, tag="bank")
+            for k in range(BANKS):
+                x_times_w(rope_bank[:, k, :], GROUP_COLS * g + BANK_COLS * k + NOPE, window)
+            turned_rope[g] = rope_bank
+
+        def multiply_turned_plain(g):
+            entries = banks.tile([P, GROUP_HEADS, P], F32, tag="bank")
+            for h in range(GROUP_HEADS):
+                col = GROUP_COLS * g + HEAD * h
+                nc.tensor.matmul_mx(
+                    out=entries[:, h, :],
+                    lhsT=w_words[:, 2 * col : 2 * (col + NOPE)].bitcast(FP4X4),
+                    lhsT_scale=w_scales[:, col : col + NOPE],
+                    rhs=x_codes[:].bitcast(FP8X4),
+                    rhs_scale=x_scales[:],
+                    start=True,
+                    stop=True,
+                )
+            turned[g] = entries
+
+        def add_bias_on_scalar(g):
+            biased = group.tile([P, GROUP_HEADS, P], F32, name="biased")
+            for h in range(GROUP_HEADS):
+                column = GROUP_HEADS * (g - TURNED[0]) + h
+                nc.scalar.activation(
+                    out=biased[:, h, :],
+                    in_=turned[g][:, h, :],
+                    func=mybir.ActivationFunctionType.Identity,
+                    bias=b_col[:, column, 0:1],
+                    scale=1.0,
+                )
+            turned_sb[g] = biased
+
+        def turn_back(g):
+            back = banks.tile([P, GROUP_HEADS, NOPE], F32, tag="bank")
+            for h in range(GROUP_HEADS):
+                nc.tensor.transpose(back[:, h, :], turned_sb[g][:, h, :], identity[:])
+            turned_back[g] = back
+
         multiply(0)
         multiply(1)
-        window = 2 * ROPE + NOPE
-        turned_rope = banks.tile([P, BANKS, window], F32, tag="bank")
-        for k in range(BANKS):
-            x_times_w(turned_rope[:, k, :], GROUP_COLS * TURNED + BANK_COLS * k + NOPE, window)
+        multiply_turned_rotated(1)
         biases.append(spread_bias(3))
         tables_ps = table_bank.tile([P, 2, ROPE], F32)
         nc.tensor.matmul(
@@ -185,32 +228,15 @@ def tile_mla_pb_s_kernel(tc, x, wq_w_words, wq_w_scales, wq_b, cos, sin, out):
             start=True,
             stop=True,
         )
-        turned = banks.tile([P, GROUP_HEADS, P], F32, tag="bank")
-        for h in range(GROUP_HEADS):
-            col = GROUP_COLS * TURNED + HEAD * h
-            nc.tensor.matmul_mx(
-                out=turned[:, h, :],
-                lhsT=w_words[:, 2 * col : 2 * (col + NOPE)].bitcast(FP4X4),
-                lhsT_scale=w_scales[:, col : col + NOPE],
-                rhs=x_codes[:].bitcast(FP8X4),
-                rhs_scale=x_scales[:],
-                start=True,
-                stop=True,
-            )
-        turned_sb = keep.tile([P, GROUP_HEADS, P], F32)
-        for h in range(GROUP_HEADS):
-            nc.scalar.activation(
-                out=turned_sb[:, h, :],
-                in_=turned[:, h, :],
-                func=mybir.ActivationFunctionType.Identity,
-                bias=b_col[:, h, 0:1],
-                scale=1.0,
-            )
-        for i in (4, 5, 6, 7):
-            multiply(i)
-        turned_back = banks.tile([P, GROUP_HEADS, NOPE], F32, tag="bank")
-        for h in range(GROUP_HEADS):
-            nc.tensor.transpose(turned_back[:, h, :], turned_sb[:, h, :], identity[:])
+        multiply_turned_plain(1)
+        multiply_turned_plain(2)
+        add_bias_on_scalar(1)
+        add_bias_on_scalar(2)
+        multiply_turned_rotated(2)
+        multiply(6)
+        multiply(7)
+        turn_back(1)
+        turn_back(2)
 
         pair_view = "p h (j t) -> p h j t"
         qs = [group.tile([P, GROUP_HEADS, HEAD], F32, name="q") for g in range(GROUPS)]
@@ -227,14 +253,17 @@ def tile_mla_pb_s_kernel(tc, x, wq_w_words, wq_w_scales, wq_b, cos, sin, out):
                 op=ADD,
             )
 
-        def add_bias_turned():
+        def add_bias_turned(g):
             ends = "p (k s) c -> p k s c"
             nc.vector.tensor_tensor(
-                out=qs[TURNED][:, :, NOPE:HEAD].rearrange(ends, s=2),
-                in0=turned_rope[:].rearrange("p k (s c) -> p k s c", c=ROPE)[:, :, 0:4:3, :],
-                in1=biases[TURNED][:, :, NOPE:HEAD].rearrange(ends, s=2),
+                out=qs[g][:, :, NOPE:HEAD].rearrange(ends, s=2),
+                in0=turned_rope[g][:].rearrange("p k (s c) -> p k s c", c=ROPE)[:, :, 0:4:3, :],
+                in1=biases[g][:, :, NOPE:HEAD].rearrange(ends, s=2),
                 op=ADD,
             )
+
+        def copy_back(g):
+            nc.scalar.copy(out=qs[g][:, :, 0:NOPE], in_=turned_back[g][:])
 
         def multiply_tables(engine, both_tables, g, heads):
             shape = [P, heads.stop - heads.start, 2, ROPE]
@@ -262,18 +291,18 @@ def tile_mla_pb_s_kernel(tc, x, wq_w_words, wq_w_scales, wq_b, cos, sin, out):
 
         add_bias(0)
         add_bias(1)
-        add_bias_turned()
+        add_bias_turned(1)
         multiply_tables(nc.vector, tables_ps[:], 0, whole)
         finish_sum(nc.gpsimd, 0, whole)
         store(0, whole)
-        multiply_tables(nc.vector, tables_ps[:], TURNED, whole)
-        nc.scalar.copy(out=qs[TURNED][:, :, 0:NOPE], in_=turned_back[:])
-        finish_sum(nc.gpsimd, TURNED, whole)
-        store(TURNED, whole)
-        add_bias(4)
-        add_bias(5)
+        multiply_tables(nc.vector, tables_ps[:], 1, whole)
+        copy_back(1)
+        finish_sum(nc.gpsimd, 1, whole)
+        store(1, whole)
+        add_bias_turned(2)
         add_bias(6, NOPE, HEAD)
         multiply_tables(nc.vector, tables_ps[:], 2, whole)
+        copy_back(2)
         finish_sum(nc.gpsimd, 2, whole)
         store(2, whole)
         add_bias(7, NOPE, HEAD)

@@ -36,6 +36,7 @@ WORD_PLANES = GROUP_WORDS // P
 
 BIAS_AHEAD = 2
 
+WORDS = COLS // 2 // P
 WARM_PASSES = 4
 TURNED = (1, 2)
 
@@ -67,6 +68,10 @@ def tile_mla_pb_s_kernel(tc, x, wq_w_words, wq_w_scales, wq_b, cos, sin, out):
         identity = keep.tile([P, P], F32)
         nc.vector.memset(identity[:], 0.0)
         make_identity(nc, identity[:], nomemset=True)
+        b_rows = keep.tile([P, P], BF16)
+        nc.vector.memset(b_rows[:].bitcast(F32), 0.0)
+        identity_bf = keep.tile([P, P], BF16)
+        make_identity(nc, identity_bf[:])
 
         cos_sin_bf = keep.tile([P, 2, HALF], BF16)
 
@@ -80,10 +85,8 @@ def tile_mla_pb_s_kernel(tc, x, wq_w_words, wq_w_scales, wq_b, cos, sin, out):
         x_sb = keep.tile([P, DIM], BF16)
         nc.sync.dma_start(out=x_sb[:], in_=x_rows)
 
-        b_sb = keep.tile([P, GROUPS, 2 * WORD_PLANES], BF16)
-        nc.scalar.dma_start(
-            out=b_sb[:], in_=wq_b.rearrange("(g p e) -> p g e", g=GROUPS, p=P)
-        )
+        b_sb = keep.tile([P, 2 * WORDS], BF16)
+        nc.scalar.dma_start(out=b_sb[:], in_=wq_b.rearrange("(p e) -> p e", p=P))
 
         for r in range(4):
             nc.sync.dma_start(
@@ -91,7 +94,6 @@ def tile_mla_pb_s_kernel(tc, x, wq_w_words, wq_w_scales, wq_b, cos, sin, out):
                 in_=scale_rows[r:16:4, :].bitcast(I32),
             )
 
-        b_col = keep.tile([P, len(TURNED) * GROUP_HEADS, 2], BF16)
         w_words = keep.tile([P, 2 * COLS], U8, align_bytes=64)
         for half in range(2):
             half_bytes = slice(COLS * half, COLS * (half + 1))
@@ -101,13 +103,9 @@ def tile_mla_pb_s_kernel(tc, x, wq_w_words, wq_w_scales, wq_b, cos, sin, out):
             )
             if half == 0:
                 load_table(nc.sync, 1, sin)
-                with nc.allow_non_contiguous_dma(reason="one bias entry to a partition"):
-                    nc.sync.dma_start(
-                        out=b_col[:, :, 0:1],
-                        in_=wq_b.rearrange("(h d) -> d h", d=HEAD)[
-                            0:NOPE, GROUP_HEADS * TURNED[0] : GROUP_HEADS * (TURNED[-1] + 1)
-                        ].unsqueeze(2),
-                    )
+                nc.sync.dma_start(
+                    out=b_rows[0:HEADS, :], in_=wq_b.rearrange("(h d) -> h d", d=HEAD)[:, 0:NOPE]
+                )
 
         tables = keep.tile([P, 2, HALF, 2], F32)
         nc.scalar.copy(
@@ -129,21 +127,30 @@ def tile_mla_pb_s_kernel(tc, x, wq_w_words, wq_w_scales, wq_b, cos, sin, out):
         )
 
         b_words = b_sb[:].bitcast(F32)
-
-        def spread_bias(g):
-            spread = banks.tile([P, WORD_PLANES, P], F32, tag="bank")
-            for w in range(WORD_PLANES):
+        spreads = []
+        for k in range(WORDS // 4):
+            spread = banks.tile([P, 4, P], F32, tag="bank")
+            for w in range(4):
                 nc.tensor.transpose(
-                    spread[:, w, :], b_words[:, g, w : w + 1].to_broadcast([P, P]), identity[:]
+                    spread[:, w, :],
+                    b_words[:, 4 * k + w : 4 * k + w + 1].to_broadcast([P, P]),
+                    identity[:],
                 )
+            spreads.append(spread)
+
+        def copy_bias(g):
             bias = group.tile([P, GROUP_HEADS, HEAD], BF16)
-            nc.scalar.copy(
-                out=bias[:]
+            words = (
+                bias[:]
                 .rearrange("p h d -> p (h d)")
                 .bitcast(F32)
-                .rearrange("p (n w) -> p n w", w=WORD_PLANES),
-                in_=spread[:].rearrange("p w n -> p n w"),
+                .rearrange("p (n w) -> p n w", w=WORDS)
             )
+            for k in range(WORDS // 4):
+                nc.scalar.copy(
+                    out=words[:, :, 4 * k : 4 * (k + 1)],
+                    in_=spreads[k][:, :, 32 * g : 32 * (g + 1)].rearrange("p w n -> p n w"),
+                )
             return bias
 
         def x_times_w(acc_cols, col, width):
@@ -166,7 +173,7 @@ def tile_mla_pb_s_kernel(tc, x, wq_w_words, wq_w_scales, wq_b, cos, sin, out):
                 x_times_w(acc_cols[:, offset : offset + width], BANK_COLS * i + offset, width)
             accs[i] = acc
 
-        biases = [spread_bias(0), spread_bias(1), spread_bias(2)]
+        biases = [copy_bias(0), copy_bias(1)]
         nc.scalar.copy(out=tables[:, 1, :, 0], in_=cos_sin_bf[:, 1, :])
         nc.scalar.mul(out=tables[:, 1, :, 1], in_=cos_sin_bf[:, 1, :], mul=-1.0)
 
@@ -200,12 +207,12 @@ def tile_mla_pb_s_kernel(tc, x, wq_w_words, wq_w_scales, wq_b, cos, sin, out):
         def add_bias_on_scalar(g):
             biased = group.tile([P, GROUP_HEADS, P], F32, name="biased")
             for h in range(GROUP_HEADS):
-                column = GROUP_HEADS * (g - TURNED[0]) + h
+                column = GROUP_HEADS * g + h
                 nc.scalar.activation(
                     out=biased[:, h, :],
                     in_=turned[g][:, h, :],
                     func=mybir.ActivationFunctionType.Identity,
-                    bias=b_col[:, column, 0:1],
+                    bias=b_col[:, column : column + 1],
                     scale=1.0,
                 )
             turned_sb[g] = biased
@@ -219,7 +226,12 @@ def tile_mla_pb_s_kernel(tc, x, wq_w_words, wq_w_scales, wq_b, cos, sin, out):
         multiply(0)
         multiply(1)
         multiply_turned_rotated(1)
-        biases.append(spread_bias(3))
+        biases.append(copy_bias(2))
+        biases.append(copy_bias(3))
+        b_col_ps = banks.tile([P, P], BF16, tag="bank")
+        nc.tensor.transpose(b_col_ps[:], b_rows[:], identity_bf[:])
+        b_col = keep.tile([P, HEADS], F32)
+        nc.scalar.copy(out=b_col[:], in_=b_col_ps[:, 0:HEADS])
         tables_ps = table_bank.tile([P, 2, ROPE], F32)
         nc.tensor.matmul(
             out=tables_ps[:].rearrange("p w c -> p (w c)"),

@@ -72,14 +72,23 @@ def tile_mla_pb_s_kernel(tc, x, wq_w_words, wq_w_scales, wq_b, cos, sin, out):
         nc.vector.memset(b_rows[:].bitcast(F32), 0.0)
         identity_bf = keep.tile([P, P], BF16)
         make_identity(nc, identity_bf[:])
+        repeat = keep.tile([P, P], F32)
+        nc.vector.memset(repeat[:], 0.0)
+        make_identity(nc, repeat[:], nomemset=True)
+        nc.gpsimd.affine_select(
+            out=repeat[:],
+            in_=repeat[:],
+            compare_op=mybir.AluOpType.not_equal,
+            fill=1.0,
+            base=SEQ,
+            pattern=[[-1, P]],
+            channel_multiplier=1,
+        )
 
-        cos_sin_bf = keep.tile([P, 2, HALF], BF16)
+        cos_sin_bf = keep.tile([SEQ, 2, HALF], BF16)
 
         def load_table(queue, plane, table):
-            queue.dma_start(
-                out=cos_sin_bf[:, plane, :],
-                in_=table.unsqueeze(0).to_broadcast([BATCH, SEQ, HALF]),
-            )
+            queue.dma_start(out=cos_sin_bf[:, plane, :], in_=table)
 
         load_table(nc.scalar, 0, cos)
         x_sb = keep.tile([P, DIM], BF16)
@@ -108,8 +117,10 @@ def tile_mla_pb_s_kernel(tc, x, wq_w_words, wq_w_scales, wq_b, cos, sin, out):
                 )
 
         tables = keep.tile([P, 2, HALF, 2], F32)
+        nc.vector.memset(tables[:], 0.0)
         nc.scalar.copy(
-            out=tables[:, 0, :, :], in_=cos_sin_bf[:, 0, :].unsqueeze(2).to_broadcast([P, HALF, 2])
+            out=tables[0:SEQ, 0, :, :],
+            in_=cos_sin_bf[:, 0, :].unsqueeze(2).to_broadcast([SEQ, HALF, 2]),
         )
 
         x_words = x_sb[:].bitcast(F32)
@@ -174,8 +185,8 @@ def tile_mla_pb_s_kernel(tc, x, wq_w_words, wq_w_scales, wq_b, cos, sin, out):
             accs[i] = acc
 
         biases = [copy_bias(0), copy_bias(1)]
-        nc.scalar.copy(out=tables[:, 1, :, 0], in_=cos_sin_bf[:, 1, :])
-        nc.scalar.mul(out=tables[:, 1, :, 1], in_=cos_sin_bf[:, 1, :], mul=-1.0)
+        nc.scalar.copy(out=tables[0:SEQ, 1, :, 0], in_=cos_sin_bf[:, 1, :])
+        nc.scalar.mul(out=tables[0:SEQ, 1, :, 1], in_=cos_sin_bf[:, 1, :], mul=-1.0)
 
         window = 2 * ROPE + NOPE
         turned_rope = {}
@@ -235,7 +246,7 @@ def tile_mla_pb_s_kernel(tc, x, wq_w_words, wq_w_scales, wq_b, cos, sin, out):
         tables_ps = table_bank.tile([P, 2, ROPE], F32)
         nc.tensor.matmul(
             out=tables_ps[:].rearrange("p w c -> p (w c)"),
-            lhsT=identity[:],
+            lhsT=repeat[:],
             rhs=tables[:].rearrange("p w j t -> p (w j t)"),
             start=True,
             stop=True,

@@ -96,6 +96,8 @@ def tile_mla_pb_s_kernel(tc, x, wq_w_words, wq_w_scales, wq_b, cos, sin, out):
 
         b_sb = keep.tile([P, 2 * WORDS], BF16)
         nc.scalar.dma_start(out=b_sb[:], in_=wq_b.rearrange("(p e) -> p e", p=P))
+        first_copy = keep.tile([P, 1], F32)
+        nc.scalar.copy(out=first_copy[:], in_=zeros[:, 0:1])
 
         for r in range(4):
             nc.sync.dma_start(

from contextlib import ExitStack

import concourse.mybir as mybir
from concourse.masks import make_identity

F32 = mybir.dt.float32
BF16 = mybir.dt.bfloat16
I32 = mybir.dt.int32
U32 = mybir.dt.uint32
U8 = mybir.dt.uint8
FP8X4 = mybir.dt.float8_e4m3fn_x4
FP4X4 = mybir.dt.float4_e2m1fn_x4
ADD = mybir.AluOpType.add
MULT = mybir.AluOpType.mult

P = 128
BATCH = 2
SEQ = 64
DIM = 512
HEADS = 16
NOPE = 128
ROPE = 64
HALF = ROPE // 2
HEAD = NOPE + ROPE
COLS = HEADS * HEAD

GROUPS = 4
GROUP_HEADS = HEADS // GROUPS
GROUP_COLS = GROUP_HEADS * HEAD
BANK_HEADS = 2
BANK_COLS = BANK_HEADS * HEAD
BANKS = GROUP_HEADS // BANK_HEADS
PASSES = ((0, 256), (256, 128))
GROUP_WORDS = GROUP_COLS // 2
WORD_PLANES = GROUP_WORDS // P

BIAS_AHEAD = 2

WORDS = COLS // 2 // P
WARM_PASSES = 4
TURNED = (1, 2)

FLOPS = 2 * P * DIM * COLS


def tile_mla_pb_s_kernel(tc, x, wq_w_words, wq_w_scales, wq_b, cos, sin, out):
    nc = tc.nc
    x_rows = x.rearrange("b s k -> (b s) k")
    w_rows = wq_w_words.rearrange("g p c -> (g p) c")
    scale_rows = wq_w_scales.rearrange("g q n -> (g q) n")
    out_rows = out.rearrange("b s h d -> (b s) (h d)")

    with ExitStack() as stack:
        keep = stack.enter_context(tc.tile_pool(name="keep", bufs=1))
        group = stack.enter_context(tc.tile_pool(name="group", bufs=GROUPS))
        banks = stack.enter_context(tc.psum_pool(name="banks", bufs=7))
        table_bank = stack.enter_context(tc.psum_pool(name="table_bank", bufs=1))
        stack.enter_context(tc.manual_schedule())

        zeros = keep.tile([P, P], F32)
        nc.gpsimd.memset(zeros[:], 0.0)
        warm = banks.tile([P, P], F32, tag="bank")
        for i in range(WARM_PASSES):
            nc.tensor.matmul(out=warm[:], lhsT=zeros[:], rhs=zeros[:], start=True, stop=True)

        w_scales = keep.tile([P, COLS], U8, align_bytes=64)
        nc.vector.memset(w_scales[:].bitcast(I32), 0)
        identity = keep.tile([P, P], F32)
        nc.vector.memset(identity[:], 0.0)
        make_identity(nc, identity[:], nomemset=True)
        b_rows = keep.tile([P, P], BF16)
        nc.vector.memset(b_rows[:].bitcast(F32), 0.0)
        identity_bf = keep.tile([P, P], BF16)
        make_identity(nc, identity_bf[:])
        repeat = keep.tile([P, P], F32)
        nc.vector.memset(repeat[:], 0.0)
        make_identity(nc, repeat[:], nomemset=True)
        nc.gpsimd.affine_select(
            out=repeat[:],
            in_=repeat[:],
            compare_op=mybir.AluOpType.not_equal,
            fill=1.0,
            base=SEQ,
            pattern=[[-1, P]],
            channel_multiplier=1,
        )

        cos_sin_bf = keep.tile([SEQ, 2, HALF], BF16)

        def load_table(queue, plane, table):
            queue.dma_start(out=cos_sin_bf[:, plane, :], in_=table)

        load_table(nc.scalar, 0, cos)
        x_sb = keep.tile([P, DIM], BF16)
        nc.sync.dma_start(out=x_sb[:], in_=x_rows)

        b_sb = keep.tile([P, 2 * WORDS], BF16)
        nc.scalar.dma_start(out=b_sb[:], in_=wq_b.rearrange("(p e) -> p e", p=P))
        first_copy = keep.tile([P, 1], F32)
        nc.scalar.copy(out=first_copy[:], in_=zeros[:, 0:1])

        for r in range(4):
            nc.sync.dma_start(
                out=w_scales[r:P:32, :].bitcast(I32),
                in_=scale_rows[r:16:4, :].bitcast(I32),
            )

        w_words = keep.tile([P, 2 * COLS], U8, align_bytes=64)
        for half in range(2):
            half_bytes = slice(COLS * half, COLS * (half + 1))
            nc.sync.dma_start(
                out=w_words[:, half_bytes].bitcast(I32),
                in_=w_rows[:, half_bytes].bitcast(I32),
            )
            if half == 0:
                load_table(nc.sync, 1, sin)
                nc.sync.dma_start(
                    out=b_rows[0:HEADS, :], in_=wq_b.rearrange("(h d) -> h d", d=HEAD)[:, 0:NOPE]
                )

        tables = keep.tile([P, 2, HALF, 2], F32)
        nc.vector.memset(tables[:], 0.0)
        nc.scalar.copy(
            out=tables[0:SEQ, 0, :, :],
            in_=cos_sin_bf[:, 0, :].unsqueeze(2).to_broadcast([SEQ, HALF, 2]),
        )

        x_words = x_sb[:].bitcast(F32)
        xt = banks.tile([P, 2, P], F32, tag="bank")
        for u in range(2):
            nc.tensor.transpose(xt[:, u, :], x_words[:, u : DIM // 2 : 2], identity[:])
        x_grouped = keep.tile([P, P, 4], BF16, align_bytes=64)
        nc.scalar.copy(out=x_grouped[:].bitcast(F32), in_=xt[:].rearrange("p u r -> p r u"))
        x_codes = keep.tile([P, P], U32, align_bytes=64)
        x_scales = keep.tile([P, P], U8, align_bytes=64)
        nc.vector.quantize_mx(
            out=x_codes[:].bitcast(FP8X4),
            scales=x_scales[:],
            in_=x_grouped[:].rearrange("p r t -> p (r t)"),
        )

        b_words = b_sb[:].bitcast(F32)
        spreads = []
        for k in range(WORDS // 4):
            spread = banks.tile([P, 4, P], F32, tag="bank")
            for w in range(4):
                nc.tensor.transpose(
                    spread[:, w, :],
                    b_words[:, 4 * k + w : 4 * k + w + 1].to_broadcast([P, P]),
                    identity[:],
                )
            spreads.append(spread)

        def copy_bias(g):
            bias = group.tile([P, GROUP_HEADS, HEAD], BF16)
            words = (
                bias[:]
                .rearrange("p h d -> p (h d)")
                .bitcast(F32)
                .rearrange("p (n w) -> p n w", w=WORDS)
            )
            for k in range(WORDS // 4):
                nc.scalar.copy(
                    out=words[:, :, 4 * k : 4 * (k + 1)],
                    in_=spreads[k][:, :, 32 * g : 32 * (g + 1)].rearrange("p w n -> p n w"),
                )
            return bias

        def x_times_w(acc_cols, col, width):
            nc.tensor.matmul_mx(
                out=acc_cols,
                lhsT=x_codes[:].bitcast(FP8X4),
                lhsT_scale=x_scales[:],
                rhs=w_words[:, 2 * col : 2 * (col + width)].bitcast(FP4X4),
                rhs_scale=w_scales[:, col : col + width],
                start=True,
                stop=True,
            )

        accs = {}

        def multiply(i):
            acc = banks.tile([P, BANK_HEADS, HEAD], F32, tag="bank")
            acc_cols = acc[:].rearrange("p h d -> p (h d)")
            for offset, width in PASSES:
                x_times_w(acc_cols[:, offset : offset + width], BANK_COLS * i + offset, width)
            accs[i] = acc

        biases = [copy_bias(0), copy_bias(1)]
        nc.scalar.copy(out=tables[0:SEQ, 1, :, 0], in_=cos_sin_bf[:, 1, :])
        nc.scalar.mul(out=tables[0:SEQ, 1, :, 1], in_=cos_sin_bf[:, 1, :], mul=-1.0)

        window = 2 * ROPE + NOPE
        turned_rope = {}
        turned = {}
        turned_sb = {}
        turned_back = {}

        def multiply_turned_rotated(g):
            rope_bank = banks.tile([P, BANKS, window], F32, tag="bank")
            for k in range(BANKS):
                x_times_w(rope_bank[:, k, :], GROUP_COLS * g + BANK_COLS * k + NOPE, window)
            turned_rope[g] = rope_bank

        def multiply_turned_plain(g):
            entries = banks.tile([P, GROUP_HEADS, P], F32, tag="bank")
            for h in range(GROUP_HEADS):
                col = GROUP_COLS * g + HEAD * h
                nc.tensor.matmul_mx(
                    out=entries[:, h, :],
                    lhsT=w_words[:, 2 * col : 2 * (col + NOPE)].bitcast(FP4X4),
                    lhsT_scale=w_scales[:, col : col + NOPE],
                    rhs=x_codes[:].bitcast(FP8X4),
                    rhs_scale=x_scales[:],
                    start=True,
                    stop=True,
                )
            turned[g] = entries

        def add_bias_on_scalar(g):
            biased = group.tile([P, GROUP_HEADS, P], F32, name="biased")
            for h in range(GROUP_HEADS):
                column = GROUP_HEADS * g + h
                nc.scalar.activation(
                    out=biased[:, h, :],
                    in_=turned[g][:, h, :],
                    func=mybir.ActivationFunctionType.Identity,
                    bias=b_col[:, column : column + 1],
                    scale=1.0,
                )
            turned_sb[g] = biased

        def turn_back(g):
            back = banks.tile([P, GROUP_HEADS, NOPE], F32, tag="bank")
            for h in range(GROUP_HEADS):
                nc.tensor.transpose(back[:, h, :], turned_sb[g][:, h, :], identity[:])
            turned_back[g] = back

        multiply(0)
        multiply(1)
        multiply_turned_rotated(1)
        biases.append(copy_bias(2))
        biases.append(copy_bias(3))
        b_col_ps = banks.tile([P, P], BF16, tag="bank")
        nc.tensor.transpose(b_col_ps[:], b_rows[:], identity_bf[:])
        b_col = keep.tile([P, HEADS], F32)
        nc.scalar.copy(out=b_col[:], in_=b_col_ps[:, 0:HEADS])
        tables_ps = table_bank.tile([P, 2, ROPE], F32)
        nc.tensor.matmul(
            out=tables_ps[:].rearrange("p w c -> p (w c)"),
            lhsT=repeat[:],
            rhs=tables[:].rearrange("p w j t -> p (w j t)"),
            start=True,
            stop=True,
        )
        multiply_turned_plain(1)
        multiply_turned_plain(2)
        add_bias_on_scalar(1)
        add_bias_on_scalar(2)
        multiply_turned_rotated(2)
        multiply(6)
        multiply(7)
        turn_back(1)
        turn_back(2)

        pair_view = "p h (j t) -> p h j t"
        qs = [group.tile([P, GROUP_HEADS, HEAD], F32, name="q") for g in range(GROUPS)]
        products = [group.tile([P, GROUP_HEADS, 2, ROPE], F32, name="both") for g in range(GROUPS)]
        whole = slice(0, GROUP_HEADS)
        halves = (slice(0, BANK_HEADS), slice(BANK_HEADS, GROUP_HEADS))

        def add_bias(i, first=0, last=HEAD):
            g, bank = divmod(i, BANKS)
            nc.vector.tensor_tensor(
                out=qs[g][:, halves[bank], first:last],
                in0=accs[i][:, :, first:last],
                in1=biases[g][:, halves[bank], first:last],
                op=ADD,
            )

        def add_bias_turned(g):
            ends = "p (k s) c -> p k s c"
            nc.vector.tensor_tensor(
                out=qs[g][:, :, NOPE:HEAD].rearrange(ends, s=2),
                in0=turned_rope[g][:].rearrange("p k (s c) -> p k s c", c=ROPE)[:, :, 0:4:3, :],
                in1=biases[g][:, :, NOPE:HEAD].rearrange(ends, s=2),
                op=ADD,
            )

        def copy_back(g):
            nc.scalar.copy(out=qs[g][:, :, 0:NOPE], in_=turned_back[g][:])

        def multiply_tables(engine, both_tables, g, heads):
            shape = [P, heads.stop - heads.start, 2, ROPE]
            engine.tensor_tensor(
                out=products[g][:, heads, :, :],
                in0=qs[g][:, heads, NOPE:HEAD].unsqueeze(2).to_broadcast(shape),
                in1=both_tables.unsqueeze(1).to_broadcast(shape),
                op=MULT,
            )

        def finish_sum(engine, g, heads):
            engine.tensor_tensor(
                out=qs[g][:, heads, NOPE:HEAD].rearrange(pair_view, t=2),
                in0=products[g][:, heads, 0, :].rearrange(pair_view, t=2),
                in1=products[g][:, heads, 1, :].rearrange(pair_view, t=2)[:, :, :, ::-1],
                op=ADD,
            )

        def store(g, heads):
            first = GROUP_COLS * g + HEAD * heads.start
            nc.sync.dma_start(
                out=out_rows[:, first : first + HEAD * (heads.stop - heads.start)],
                in_=qs[g][:, heads, :].rearrange("p h d -> p (h d)"),
            )

        add_bias(0)
        add_bias(1)
        add_bias_turned(1)
        multiply_tables(nc.vector, tables_ps[:], 0, whole)
        finish_sum(nc.gpsimd, 0, whole)
        store(0, whole)
        multiply_tables(nc.vector, tables_ps[:], 1, whole)
        copy_back(1)
        finish_sum(nc.gpsimd, 1, whole)
        store(1, whole)
        add_bias_turned(2)
        add_bias(6, NOPE, HEAD)
        multiply_tables(nc.vector, tables_ps[:], 2, whole)
        copy_back(2)
        finish_sum(nc.gpsimd, 2, whole)
        store(2, whole)
        add_bias(7, NOPE, HEAD)
        add_bias(6, 0, NOPE)
        multiply_tables(nc.vector, tables_ps[:], 3, whole)
        finish_sum(nc.gpsimd, 3, halves[0])
        add_bias(7, 0, NOPE)
        finish_sum(nc.vector, 3, halves[1])
        store(3, halves[0])
        store(3, halves[1])
